import numpy as np
import ml_dtypes


def mxq(x, axis, fmt="e4m3"):
    dtype, down = {"e4m3": (ml_dtypes.float8_e4m3fn, 7), "e5m2": (ml_dtypes.float8_e5m2, 14)}[fmt]
    v = np.moveaxis(np.asarray(x, np.float32).astype(ml_dtypes.bfloat16).astype(np.float64), axis, -1)
    blocks = v.reshape(v.shape[:-1] + (-1, 32))
    amax = np.abs(blocks).max(-1, keepdims=True)
    byte = np.maximum(np.where(amax > 0, np.frexp(amax)[1] - 1 + 127, 0) - down, 1)
    scale = np.exp2(byte - 127.0)
    codes = (blocks / scale).astype(np.float32).astype(dtype).astype(np.float64)
    return np.moveaxis((codes * scale).reshape(v.shape), -1, axis)


WIDE = False


def mx_kscale(k):
    if not WIDE:
        return np.ones(k)
    levels = np.array([10, -10, 5, -5, 0])
    if k % 512:
        return np.exp2(np.random.permutation(np.resize(levels, k // 32))).repeat(32)
    a = np.empty((k // 512, 16))
    for p in range(k // 512):
        a[p, :8] = np.random.permutation(np.resize(levels, 8))
        for g in range(8):
            far = levels[np.abs(levels - a[p, g]) >= 10]
            a[p, g + 8] = far[np.random.randint(len(far))]
    return np.exp2(a.ravel()).repeat(32)


BF16 = ml_dtypes.bfloat16


def bf(x):
    return np.asarray(x, np.float32).astype(BF16)


def f64(x):
    return np.asarray(x).astype(np.float64)


E2M1 = np.array([0.0, 0.5, 1.0, 1.5, 2.0, 3.0, 4.0, 6.0, -0.0, -0.5, -1.0, -1.5, -2.0, -3.0, -4.0, -6.0])


def pack_weight(w, fmt):
    k, n = w.shape
    w = f64(bf(w)).reshape(k // 32, 32, n)
    amax = np.abs(w).max(1)
    if fmt == "e4m3":
        byte = np.frexp(amax)[1] - 1 + 127 - 7
    else:
        mant, ex = np.frexp(amax / 6.0)
        byte = np.where(mant > 0.5, ex, ex - 1) + 127
    byte = np.clip(np.where(amax > 0, byte, 1), 1, 254)
    scaled = (w * np.exp2(127.0 - byte)[:, None, :]).reshape(k, n).astype(np.float32)
    by_word = np.ascontiguousarray(scaled.reshape(k // 512, 128, 4, n).transpose(0, 1, 3, 2))
    if fmt == "e4m3":
        words = by_word.astype(ml_dtypes.float8_e4m3fn).view(np.uint8)
    else:
        c = by_word.astype(ml_dtypes.float4_e2m1fn).view(np.uint8) & 0xF
        words = c[..., 0::2] | (c[..., 1::2] << 4)
    return np.ascontiguousarray(words), np.ascontiguousarray(byte.astype(np.uint8).reshape(k // 512, 16, n))


def unpack_weight(words, scales, fmt):
    g, p, n, _ = words.shape
    if fmt == "e4m3":
        vals = np.ascontiguousarray(words).view(ml_dtypes.float8_e4m3fn).astype(np.float64)
    else:
        nib = np.empty((g, p, n, 4), np.uint8)
        nib[..., 0::2] = words & 0xF
        nib[..., 1::2] = words >> 4
        vals = E2M1[nib]
    vals = vals * np.repeat(np.exp2(scales.astype(np.float64) - 127.0), 8, axis=1)[..., None]
    return vals.transpose(0, 1, 3, 2).reshape(g * 512, n)


B, C, CK, H, W = 32, 512, 512, 16, 16
N = H * W


def draw0():
    s, t = mx_kscale(C), mx_kscale(CK)
    x = bf(np.random.standard_normal((B, C, H, W)) * s[None, :, None, None])
    Wq = np.random.standard_normal((CK, C)) / np.sqrt(C) / s[None, :] * t[:, None]
    Wq_words, Wq_scales = pack_weight(Wq.T, "e4m3")
    bq = bf(np.random.standard_normal(CK) * 0.3 * t)
    Wk = np.random.standard_normal((CK, C)) / np.sqrt(C) / s[None, :] / t[:, None]
    Wk_words, Wk_scales = pack_weight(Wk.T, "e4m3")
    return {
        "x": x,
        "Wq_words": Wq_words,
        "Wq_scales": Wq_scales,
        "bq": bq,
        "Wk_words": Wk_words,
        "Wk_scales": Wk_scales,
        "bk": bf(np.random.standard_normal(CK) * 0.3 / t),
        "fg_sim": bf(np.random.uniform(size=(B, N, N))),
    }


def core(x, Wq_words, Wq_scales, bq, Wk_words, Wk_scales, bk, fg_sim):
    xq = mxq(f64(x).reshape(B, C, N), 1, "e4m3")
    query = (unpack_weight(Wq_words, Wq_scales, "e4m3").T @ xq).transpose(0, 2, 1) + f64(bq)
    key = (unpack_weight(Wk_words, Wk_scales, "e4m3").T @ xq) + f64(bk)[None, :, None]
    sim = (mxq(query, 2, "e4m3") @ mxq(key, 1, "e4m3")) * CK ** -0.5
    return sim * f64(fg_sim)


def e4m3fn_bytes(y):
    return np.clip(np.asarray(y, np.float64), -448.0, 448.0).astype(np.float32).astype(ml_dtypes.float8_e4m3fn).view(np.uint8)


def e4m3fn_values(b):
    return np.asarray(b, np.uint8).view(ml_dtypes.float8_e4m3fn).astype(np.float64)


def setup_inputs():
    d = draw0()
    x0 = np.asarray(d['x']).astype(np.float64)
    s = (np.max(np.abs(x0), axis=(0, 2, 3), keepdims=True) / 448.0).astype(np.float32)
    out = {}
    for k, v in d.items():
        if k == 'x':
            out['x_bytes'] = e4m3fn_bytes(x0 / s.astype(np.float64))
            out['x_scale'] = s
        else:
            out[k] = v
    return out


def reference(x_bytes, x_scale, Wq_words, Wq_scales, bq, Wk_words, Wk_scales, bk, fg_sim):
    return core(e4m3fn_values(x_bytes) * x_scale.astype(np.float64), Wq_words, Wq_scales, bq, Wk_words, Wk_scales, bk, fg_sim)

@@ -1,0 +1,273 @@
+from contextlib import ExitStack
+
+import concourse.mybir as mybir
+
+B, C, N = 32, 512, 256
+P = 128
+T = 4
+H = 2
+SCALE = 512 ** -0.5
+FLOPS = 32 * (2 * 2 * 512 * 512 * 256 + 2 * 256 * 256 * 512)
+
+F32 = mybir.dt.float32
+BF16 = mybir.dt.bfloat16
+I32 = mybir.dt.int32
+U32 = mybir.dt.uint32
+U8 = mybir.dt.uint8
+FP8 = mybir.dt.float8_e4m3fn
+FP8X4 = mybir.dt.float8_e4m3fn_x4
+MULT = mybir.AluOpType.mult
+ADD = mybir.AluOpType.add
+COPY = mybir.ActivationFunctionType.Copy
+IDENT = mybir.ActivationFunctionType.Identity
+
+PREFETCH = 10
+
+
+def tile_sgan_pa_t_w8_kernel(tc, x_bytes, x_scale, Wq_words, Wq_scales, bq, Wk_words, Wk_scales, bk, fg_sim, out):
+    nc = tc.nc
+    with ExitStack() as ctx:
+        const = ctx.enter_context(tc.tile_pool(name="const", bufs=1))
+        rawp = ctx.enter_context(tc.tile_pool(name="rawp", bufs=8))
+        fgp = ctx.enter_context(tc.tile_pool(name="fgp", bufs=3))
+        planep = ctx.enter_context(tc.tile_pool(name="planep", bufs=3))
+        xintp = ctx.enter_context(tc.tile_pool(name="xintp", bufs=3))
+        xqp = ctx.enter_context(tc.tile_pool(name="xqp", bufs=3))
+        kplp = ctx.enter_context(tc.tile_pool(name="kplp", bufs=3))
+        qkp = ctx.enter_context(tc.tile_pool(name="qkp", bufs=3))
+        qkcp = ctx.enter_context(tc.tile_pool(name="qkcp", bufs=3))
+        outp = ctx.enter_context(tc.tile_pool(name="outp", bufs=4))
+        psq = ctx.enter_context(tc.psum_pool(name="psq", bufs=2))
+        psk = ctx.enter_context(tc.psum_pool(name="psk", bufs=4))
+        pso = ctx.enter_context(tc.psum_pool(name="pso", bufs=2))
+        ctx.enter_context(tc.manual_schedule())
+
+        xs = const.tile([P, T], F32, name="xs", align_bytes=64)
+        bq_b = const.tile([P, T], BF16, name="bq_b", align_bytes=64)
+        bk_b = const.tile([P, T], BF16, name="bk_b", align_bytes=64)
+        bias = const.tile([P, 2, T], F32, name="bias", align_bytes=64)
+        warm = const.tile([P, 1], F32, name="warm", align_bytes=64)
+        w_raw = const.tile([P, 2, 512], I32, name="w_raw", align_bytes=64)
+        w_codes = const.tile([P, 2, 512], I32, name="w_codes", align_bytes=64)
+        s_raw = const.tile([P, 2, 512], U8, name="s_raw", align_bytes=64)
+        w_scales = const.tile([P, 2, 512], U8, name="w_scales", align_bytes=64)
+
+        raw = {}
+        fg = {}
+
+        def load_x(m):
+            if m % 2 == 0:
+                tile = rawp.tile([P, T, 2, N], U8, name="x_codes", align_bytes=64)
+                raw[m // 2] = tile
+            nc.sync.dma_start(out=raw[m // 2][:, :, m % 2, :], in_=x_bytes[m].rearrange("(p t) h w -> p t (h w)", t=T))
+
+        def load_fg(g):
+            tile = fgp.tile([P, 4, H, N], BF16, name="fg", align_bytes=64)
+            fg[g] = tile
+            nc.sync.dma_start(out=tile[:], in_=fg_sim[4 * g : 4 * g + 4].rearrange("b (h p) m -> p b h m", p=P))
+
+        nc.scalar.dma_start(out=xs[:], in_=x_scale.rearrange("a (p t) b c -> p (a t b c)", t=T))
+        nc.scalar.dma_start(out=bk_b[:], in_=bk.rearrange("(p t) -> p t", t=T))
+        nc.scalar.dma_start(out=bq_b[:], in_=bq.rearrange("(p t) -> p t", t=T))
+        nc.vector.memset(warm[:], 0.0)
+        nc.scalar.activation(out=warm[:], in_=warm[:], func=IDENT)
+        nc.vector.memset(s_raw[:].rearrange("p w n -> p (w n)").bitcast(I32), 0)
+
+        load_x(0)
+        nc.sync.dma_start(out=w_raw[:, 1, :], in_=Wk_words[0].rearrange("p n t -> p (n t)").bitcast(I32))
+        for w, src in ((1, Wk_scales), (0, Wq_scales)):
+            for quad in range(4):
+                nc.sync.dma_start(
+                    out=s_raw[32 * quad : 32 * quad + 4, w, :].bitcast(I32),
+                    in_=src[0, 4 * quad : 4 * quad + 4, :].bitcast(I32),
+                )
+        nc.sync.dma_start(out=w_raw[:, 0, :], in_=Wq_words[0].rearrange("p n t -> p (n t)").bitcast(I32))
+        for m in range(1, PREFETCH):
+            load_x(m)
+            if m == 3:
+                load_fg(0)
+
+        planes, xint, xq, kpl, qk, qkc, ps = {}, {}, {}, {}, {}, {}, {}
+
+        def raw_plane(j, t, lo, hi):
+            return raw[j][:, t, :, :].rearrange("p b n -> p (b n)")[:, lo:hi].bitcast(FP8)
+
+        def new_planes(j):
+            tile = planep.tile([P, T, 2 * N], BF16, name="planes", align_bytes=64)
+            planes[j] = tile
+
+        def widen_s(j, t, lo=0, hi=2 * N):
+            nc.scalar.activation(out=planes[j][:, t, lo:hi], in_=raw_plane(j, t, lo, hi), func=COPY, scale=xs[:, t : t + 1])
+
+        def widen_v(j, t, lo=0, hi=2 * N):
+            nc.vector.tensor_scalar(out=planes[j][:, t, lo:hi], in0=raw_plane(j, t, lo, hi), scalar1=xs[:, t : t + 1], scalar2=None, op0=MULT)
+
+        def new_xint(j):
+            tile = xintp.tile([P, 2 * N, T], BF16, name="xint", align_bytes=64)
+            xint[j] = tile
+
+        def int_g(j, lo, hi):
+            nc.gpsimd.tensor_scalar(
+                out=xint[j][:, lo:hi, :], in0=planes[j][:, :, lo:hi].rearrange("p t n -> p n t"),
+                scalar1=1.0, scalar2=0.0, op0=MULT, op1=ADD,
+            )
+
+        def interleave(copy, dst, src):
+            copy(out=dst.rearrange("p (c i) t -> p c t i", i=4), in_=src.rearrange("p t (c i) -> p c t i", i=4))
+
+        def int_v(j, lo, hi):
+            interleave(nc.vector.tensor_copy, xint[j][:, lo:hi, :], planes[j][:, :, lo:hi])
+
+        def quant_x(j, lo=0, hi=2 * N):
+            if lo == 0:
+                codes = xqp.tile([P, 2 * N], U32, name="x_mx", align_bytes=64)
+                scales = xqp.tile([P, 2 * N], U8, name="x_mx_scales", align_bytes=64)
+                xq[j] = (codes, scales)
+            codes, scales = xq[j]
+            nc.vector.quantize_mx(
+                out=codes[:, lo:hi].bitcast(FP8X4), scales=scales[:, lo:hi],
+                in_=xint[j][:, lo:hi, :].rearrange("p n t -> p (n t)"),
+            )
+
+        def mm(dst, w, t, m, lo, hi):
+            codes, scales = xq[m // 2]
+            off = (m % 2) * N
+            nc.tensor.matmul_mx(
+                out=dst,
+                lhsT=w_codes[:, w, t * P : (t + 1) * P].bitcast(FP8X4),
+                lhsT_scale=w_scales[:, w, t * P : (t + 1) * P],
+                rhs=codes[:, off + lo : off + hi].bitcast(FP8X4),
+                rhs_scale=scales[:, off + lo : off + hi],
+                start=True, stop=True,
+            )
+
+        def pe_key(m):
+            for u in range(2):
+                bank = psk.tile([P, 2, N], F32, name="kbank")
+                ps["k", m, u] = bank
+                for e in range(2):
+                    mm(bank[:, e, :], 1, 2 * u + e, m, 0, N)
+
+        def pe_query(m):
+            for h in range(H):
+                bank = psq.tile([P, T, P], F32, name="qbank")
+                ps["q", m, h] = bank
+                for t in range(T):
+                    mm(bank[:, t, :], 0, t, m, h * P, (h + 1) * P)
+
+        def key_exit(m):
+            tile = kplp.tile([P, T, N], BF16, name="kplanes", align_bytes=64)
+            kpl[m] = tile
+            for t in range(T):
+                nc.scalar.activation(out=tile[:, t, :], in_=ps["k", m, t // 2][:, t % 2, :], func=IDENT, bias=bias[:, 1, t : t + 1])
+
+        def query_exit(m, h):
+            if h == 0:
+                tile = qkp.tile([P, 2, N, T], BF16, name="qk", align_bytes=64)
+                qk[m] = tile
+            nc.vector.tensor_tensor(
+                out=qk[m][:, 0, h * P : (h + 1) * P, :],
+                in0=ps["q", m, h][:].rearrange("p t n -> p n t"),
+                in1=bias[:, 0, :].unsqueeze(1).to_broadcast([P, P, T]),
+                op=ADD,
+            )
+
+        def key_int(copy, m, lo, hi):
+            interleave(copy, qk[m][:, 1, lo:hi, :], kpl[m][:, :, lo:hi])
+
+        def quant_qk(m):
+            codes = qkcp.tile([P, 2 * N], U32, name="qk_mx", align_bytes=64)
+            scales = qkcp.tile([P, 2 * N], U8, name="qk_mx_scales", align_bytes=64)
+            qkc[m] = (codes, scales)
+            nc.vector.quantize_mx(out=codes[:].bitcast(FP8X4), scales=scales[:], in_=qk[m][:].rearrange("p w n t -> p (w n t)"))
+
+        def pe_out(m):
+            codes, scales = qkc[m]
+            bank = pso.tile([P, H, N], F32, name="obank")
+            ps["o", m] = bank
+            for h in range(H):
+                nc.tensor.matmul_mx(
+                    out=bank[:, h, :],
+                    lhsT=codes[:, h * P : (h + 1) * P].bitcast(FP8X4),
+                    lhsT_scale=scales[:, h * P : (h + 1) * P],
+                    rhs=codes[:, N : 2 * N].bitcast(FP8X4),
+                    rhs_scale=scales[:, N : 2 * N],
+                    start=True, stop=True,
+                )
+
+        def out_exit(m):
+            tile = outp.tile([P, H, N], F32, name="res", align_bytes=64)
+            nc.vector.scalar_tensor_tensor(
+                out=tile[:], in0=ps["o", m][:], scalar=SCALE, in1=fg[m // 4][:, m % 4, :, :], op0=MULT, op1=MULT,
+            )
+            nc.sync.dma_start(out=out[m].rearrange("(h p) m -> p h m", p=P), in_=tile[:])
+
+        new_planes(0)
+        new_xint(0)
+        widen_s(0, 0, 0, N)
+        widen_s(0, 1, 0, N)
+        widen_v(0, 2, 0, N)
+        widen_v(0, 3, 0, N)
+        int_v(0, 0, N)
+        nc.vector.tensor_copy(out=w_codes[:, 1, :].rearrange("p (t m) -> p t m", t=T), in_=w_raw[:, 1, :].rearrange("p (m t) -> p t m", t=T))
+        quant_x(0, 0, N)
+        nc.vector.tensor_copy(
+            out=w_scales[:].rearrange("p w (t m) -> p w t m", t=T), in_=s_raw[:].rearrange("p w (m t) -> p w t m", t=T))
+        nc.vector.tensor_copy(out=w_codes[:, 0, :].rearrange("p (t m) -> p t m", t=T), in_=w_raw[:, 0, :].rearrange("p (m t) -> p t m", t=T))
+        nc.vector.tensor_copy(out=bias[:, 1, :], in_=bk_b[:])
+        nc.vector.tensor_copy(out=bias[:, 0, :], in_=bq_b[:])
+        for t in range(T):
+            widen_s(0, t, N, 2 * N)
+        pe_key(0)
+        pe_query(0)
+        int_v(0, N, 2 * N)
+        quant_x(0, N, 2 * N)
+        new_planes(1)
+        for t in range(T):
+            widen_v(1, t)
+        new_xint(1)
+        int_g(1, 0, P)
+        int_g(1, P, N)
+        new_planes(2)
+
+        pairs = B // 2
+        for i in range(B + 1):
+            if i + PREFETCH < B:
+                load_x(i + PREFETCH)
+            if i % 4 == 0 and i // 4 + 1 < B // 4:
+                load_fg(i // 4 + 1)
+            j = (i + 2) // 2 if i % 2 == 0 else (i + 3) // 2
+            if j < pairs:
+                off = N if i % 2 == 0 else 0
+                if i % 2 == 1:
+                    new_xint(j)
+                int_g(j, off, off + P)
+                int_g(j, off + P, off + N)
+            if i < B:
+                key_exit(i)
+                query_exit(i, 0)
+                query_exit(i, 1)
+            if i + 1 < B:
+                pe_key(i + 1)
+                pe_query(i + 1)
+            if i > 0:
+                quant_qk(i - 1)
+                pe_out(i - 1)
+            if i < B:
+                key_int(nc.vector.tensor_copy, i, 0, P)
+            if i == 0:
+                widen_s(2, 0)
+                widen_s(2, 1)
+            jw = (i + 4) // 2 if i % 2 == 0 else (i + 5) // 2
+            if jw < pairs:
+                if i % 2 == 1:
+                    new_planes(jw)
+                first = 2 if i % 2 == 0 else 0
+                widen_s(jw, first)
+                widen_s(jw, first + 1)
+            if i < B:
+                key_int(nc.scalar.copy, i, P, N)
+            if i % 2 == 0 and (i + 2) // 2 < pairs:
+                quant_x((i + 2) // 2)
+            if i > 0:
+                out_exit(i - 1)

@@ -31,8 +31,9 @@ def tile_sgan_pa_t_w8_kernel(tc, x_bytes, x_scale, Wq_words, Wq_scales, bq, Wk_w
         rawp = ctx.enter_context(tc.tile_pool(name="rawp", bufs=8))
         fgp = ctx.enter_context(tc.tile_pool(name="fgp", bufs=3))
         planep = ctx.enter_context(tc.tile_pool(name="planep", bufs=3))
-        xintp = ctx.enter_context(tc.tile_pool(name="xintp", bufs=3))
-        xqp = ctx.enter_context(tc.tile_pool(name="xqp", bufs=3))
+        xheadp = ctx.enter_context(tc.tile_pool(name="xheadp", bufs=2))
+        xintp = ctx.enter_context(tc.tile_pool(name="xintp", bufs=1))
+        xqp = ctx.enter_context(tc.tile_pool(name="xqp", bufs=4))
         kplp = ctx.enter_context(tc.tile_pool(name="kplp", bufs=3))
         qkp = ctx.enter_context(tc.tile_pool(name="qkp", bufs=3))
         qkcp = ctx.enter_context(tc.tile_pool(name="qkcp", bufs=3))
@@ -102,42 +103,39 @@ def tile_sgan_pa_t_w8_kernel(tc, x_bytes, x_scale, Wq_words, Wq_scales, bq, Wk_w
         def widen_v(j, t, lo=0, hi=2 * N):
             nc.vector.tensor_scalar(out=planes[j][:, t, lo:hi], in0=raw_plane(j, t, lo, hi), scalar1=xs[:, t : t + 1], scalar2=None, op0=MULT)
 
-        def new_xint(j):
-            tile = xintp.tile([P, 2 * N, T], BF16, name="xint", align_bytes=64)
-            xint[j] = tile
+        def image_planes(m):
+            return planes[m // 2][:, :, (m % 2) * N : (m % 2 + 1) * N]
 
-        def int_g(j, lo, hi):
+        def int_g(m):
+            tile = xintp.tile([P, N, T], BF16, name="xint", align_bytes=64)
+            xint[m] = tile
             nc.gpsimd.tensor_scalar(
-                out=xint[j][:, lo:hi, :], in0=planes[j][:, :, lo:hi].rearrange("p t n -> p n t"),
+                out=tile[:], in0=image_planes(m).rearrange("p t n -> p n t"),
                 scalar1=1.0, scalar2=0.0, op0=MULT, op1=ADD,
             )
 
         def interleave(copy, dst, src):
             copy(out=dst.rearrange("p (c i) t -> p c t i", i=4), in_=src.rearrange("p t (c i) -> p c t i", i=4))
 
-        def int_v(j, lo, hi):
-            interleave(nc.vector.tensor_copy, xint[j][:, lo:hi, :], planes[j][:, :, lo:hi])
+        def int_v(m):
+            tile = xheadp.tile([P, N, T], BF16, name="xhead", align_bytes=64)
+            xint[m] = tile
+            interleave(nc.vector.tensor_copy, tile[:], image_planes(m))
 
-        def quant_x(j, lo=0, hi=2 * N):
-            if lo == 0:
-                codes = xqp.tile([P, 2 * N], U32, name="x_mx", align_bytes=64)
-                scales = xqp.tile([P, 2 * N], U8, name="x_mx_scales", align_bytes=64)
-                xq[j] = (codes, scales)
-            codes, scales = xq[j]
-            nc.vector.quantize_mx(
-                out=codes[:, lo:hi].bitcast(FP8X4), scales=scales[:, lo:hi],
-                in_=xint[j][:, lo:hi, :].rearrange("p n t -> p (n t)"),
-            )
+        def quant_x(m):
+            codes = xqp.tile([P, N], U32, name="x_mx", align_bytes=64)
+            scales = xqp.tile([P, N], U8, name="x_mx_scales", align_bytes=64)
+            xq[m] = (codes, scales)
+            nc.vector.quantize_mx(out=codes[:].bitcast(FP8X4), scales=scales[:], in_=xint[m][:].rearrange("p n t -> p (n t)"))
 
         def mm(dst, w, t, m, lo, hi):
-            codes, scales = xq[m // 2]
-            off = (m % 2) * N
+            codes, scales = xq[m]
             nc.tensor.matmul_mx(
                 out=dst,
                 lhsT=w_codes[:, w, t * P : (t + 1) * P].bitcast(FP8X4),
                 lhsT_scale=w_scales[:, w, t * P : (t + 1) * P],
-                rhs=codes[:, off + lo : off + hi].bitcast(FP8X4),
-                rhs_scale=scales[:, off + lo : off + hi],
+                rhs=codes[:, lo:hi].bitcast(FP8X4),
+                rhs_scale=scales[:, lo:hi],
                 start=True, stop=True,
             )
 
@@ -203,14 +201,13 @@ def tile_sgan_pa_t_w8_kernel(tc, x_bytes, x_scale, Wq_words, Wq_scales, bq, Wk_w
             nc.sync.dma_start(out=out[m].rearrange("(h p) m -> p h m", p=P), in_=tile[:])
 
         new_planes(0)
-        new_xint(0)
         widen_s(0, 0, 0, N)
         widen_s(0, 1, 0, N)
         widen_v(0, 2, 0, N)
         widen_v(0, 3, 0, N)
-        int_v(0, 0, N)
+        int_v(0)
         nc.vector.tensor_copy(out=w_codes[:, 1, :].rearrange("p (t m) -> p t m", t=T), in_=w_raw[:, 1, :].rearrange("p (m t) -> p t m", t=T))
-        quant_x(0, 0, N)
+        quant_x(0)
         nc.vector.tensor_copy(
             out=w_scales[:].rearrange("p w (t m) -> p w t m", t=T), in_=s_raw[:].rearrange("p w (m t) -> p w t m", t=T))
         nc.vector.tensor_copy(out=w_codes[:, 0, :].rearrange("p (t m) -> p t m", t=T), in_=w_raw[:, 0, :].rearrange("p (m t) -> p t m", t=T))
@@ -220,41 +217,38 @@ def tile_sgan_pa_t_w8_kernel(tc, x_bytes, x_scale, Wq_words, Wq_scales, bq, Wk_w
             widen_s(0, t, N, 2 * N)
         pe_key(0)
         pe_query(0)
-        int_v(0, N, 2 * N)
-        quant_x(0, N, 2 * N)
         new_planes(1)
         for t in range(T):
             widen_v(1, t)
-        new_xint(1)
-        int_g(1, 0, P)
-        int_g(1, P, N)
+        int_g(2)
+        int_v(1)
+        quant_x(1)
         new_planes(2)
 
         pairs = B // 2
-        for i in range(B + 1):
+        for i in range(B + 2):
             if i + PREFETCH < B:
                 load_x(i + PREFETCH)
             if i % 4 == 0 and i // 4 + 1 < B // 4:
                 load_fg(i // 4 + 1)
-            j = (i + 2) // 2 if i % 2 == 0 else (i + 3) // 2
-            if j < pairs:
-                off = N if i % 2 == 0 else 0
-                if i % 2 == 1:
-                    new_xint(j)
-                int_g(j, off, off + P)
-                int_g(j, off + P, off + N)
             if i < B:
                 key_exit(i)
                 query_exit(i, 0)
                 query_exit(i, 1)
+            if i > 1:
+                out_exit(i - 2)
             if i + 1 < B:
                 pe_key(i + 1)
                 pe_query(i + 1)
-            if i > 0:
-                quant_qk(i - 1)
-                pe_out(i - 1)
             if i < B:
                 key_int(nc.vector.tensor_copy, i, 0, P)
+            if 0 < i <= B:
+                quant_qk(i - 1)
+                pe_out(i - 1)
+            if i + 2 < B:
+                quant_x(i + 2)
+            if i + 3 < B:
+                int_g(i + 3)
             if i == 0:
                 widen_s(2, 0)
                 widen_s(2, 1)
@@ -267,7 +261,3 @@ def tile_sgan_pa_t_w8_kernel(tc, x_bytes, x_scale, Wq_words, Wq_scales, bq, Wk_w
                 widen_s(jw, first + 1)
             if i < B:
                 key_int(nc.scalar.copy, i, P, N)
-            if i % 2 == 0 and (i + 2) // 2 < pairs:
-                quant_x((i + 2) // 2)
-            if i > 0:
-                out_exit(i - 1)

from contextlib import ExitStack

import concourse.mybir as mybir

B, C, N = 32, 512, 256
P = 128
T = 4
H = 2
SCALE = 512 ** -0.5
FLOPS = 32 * (2 * 2 * 512 * 512 * 256 + 2 * 256 * 256 * 512)

F32 = mybir.dt.float32
BF16 = mybir.dt.bfloat16
I32 = mybir.dt.int32
U32 = mybir.dt.uint32
U8 = mybir.dt.uint8
FP8 = mybir.dt.float8_e4m3fn
FP8X4 = mybir.dt.float8_e4m3fn_x4
MULT = mybir.AluOpType.mult
ADD = mybir.AluOpType.add
COPY = mybir.ActivationFunctionType.Copy
IDENT = mybir.ActivationFunctionType.Identity

PREFETCH = 10


def tile_sgan_pa_t_w8_kernel(tc, x_bytes, x_scale, Wq_words, Wq_scales, bq, Wk_words, Wk_scales, bk, fg_sim, out):
    nc = tc.nc
    with ExitStack() as ctx:
        const = ctx.enter_context(tc.tile_pool(name="const", bufs=1))
        rawp = ctx.enter_context(tc.tile_pool(name="rawp", bufs=8))
        fgp = ctx.enter_context(tc.tile_pool(name="fgp", bufs=3))
        planep = ctx.enter_context(tc.tile_pool(name="planep", bufs=3))
        xheadp = ctx.enter_context(tc.tile_pool(name="xheadp", bufs=2))
        xintp = ctx.enter_context(tc.tile_pool(name="xintp", bufs=1))
        xqp = ctx.enter_context(tc.tile_pool(name="xqp", bufs=4))
        kplp = ctx.enter_context(tc.tile_pool(name="kplp", bufs=3))
        qkp = ctx.enter_context(tc.tile_pool(name="qkp", bufs=3))
        qkcp = ctx.enter_context(tc.tile_pool(name="qkcp", bufs=3))
        outp = ctx.enter_context(tc.tile_pool(name="outp", bufs=4))
        psq = ctx.enter_context(tc.psum_pool(name="psq", bufs=2))
        psk = ctx.enter_context(tc.psum_pool(name="psk", bufs=4))
        pso = ctx.enter_context(tc.psum_pool(name="pso", bufs=2))
        ctx.enter_context(tc.manual_schedule())

        xs = const.tile([P, T], F32, name="xs", align_bytes=64)
        bq_b = const.tile([P, T], BF16, name="bq_b", align_bytes=64)
        bk_b = const.tile([P, T], BF16, name="bk_b", align_bytes=64)
        bias = const.tile([P, 2, T], F32, name="bias", align_bytes=64)
        warm = const.tile([P, 1], F32, name="warm", align_bytes=64)
        w_raw = const.tile([P, 2, 512], I32, name="w_raw", align_bytes=64)
        w_codes = const.tile([P, 2, 512], I32, name="w_codes", align_bytes=64)
        s_raw = const.tile([P, 2, 512], U8, name="s_raw", align_bytes=64)
        w_scales = const.tile([P, 2, 512], U8, name="w_scales", align_bytes=64)

        raw = {}
        fg = {}

        def load_x(m):
            if m % 2 == 0:
                tile = rawp.tile([P, T, 2, N], U8, name="x_codes", align_bytes=64)
                raw[m // 2] = tile
            nc.sync.dma_start(out=raw[m // 2][:, :, m % 2, :], in_=x_bytes[m].rearrange("(p t) h w -> p t (h w)", t=T))

        def load_fg(g):
            tile = fgp.tile([P, 4, H, N], BF16, name="fg", align_bytes=64)
            fg[g] = tile
            nc.sync.dma_start(out=tile[:], in_=fg_sim[4 * g : 4 * g + 4].rearrange("b (h p) m -> p b h m", p=P))

        nc.scalar.dma_start(out=xs[:], in_=x_scale.rearrange("a (p t) b c -> p (a t b c)", t=T))
        nc.scalar.dma_start(out=bk_b[:], in_=bk.rearrange("(p t) -> p t", t=T))
        nc.scalar.dma_start(out=bq_b[:], in_=bq.rearrange("(p t) -> p t", t=T))
        nc.vector.memset(warm[:], 0.0)
        nc.scalar.activation(out=warm[:], in_=warm[:], func=IDENT)
        nc.vector.memset(s_raw[:].rearrange("p w n -> p (w n)").bitcast(I32), 0)

        load_x(0)
        nc.sync.dma_start(out=w_raw[:, 1, :], in_=Wk_words[0].rearrange("p n t -> p (n t)").bitcast(I32))
        for w, src in ((1, Wk_scales), (0, Wq_scales)):
            for quad in range(4):
                nc.sync.dma_start(
                    out=s_raw[32 * quad : 32 * quad + 4, w, :].bitcast(I32),
                    in_=src[0, 4 * quad : 4 * quad + 4, :].bitcast(I32),
                )
        nc.sync.dma_start(out=w_raw[:, 0, :], in_=Wq_words[0].rearrange("p n t -> p (n t)").bitcast(I32))
        for m in range(1, PREFETCH):
            load_x(m)
            if m == 3:
                load_fg(0)

        planes, xint, xq, kpl, qk, qkc, ps = {}, {}, {}, {}, {}, {}, {}

        def raw_plane(j, t, lo, hi):
            return raw[j][:, t, :, :].rearrange("p b n -> p (b n)")[:, lo:hi].bitcast(FP8)

        def new_planes(j):
            tile = planep.tile([P, T, 2 * N], BF16, name="planes", align_bytes=64)
            planes[j] = tile

        def widen_s(j, t, lo=0, hi=2 * N):
            nc.scalar.activation(out=planes[j][:, t, lo:hi], in_=raw_plane(j, t, lo, hi), func=COPY, scale=xs[:, t : t + 1])

        def widen_v(j, t, lo=0, hi=2 * N):
            nc.vector.tensor_scalar(out=planes[j][:, t, lo:hi], in0=raw_plane(j, t, lo, hi), scalar1=xs[:, t : t + 1], scalar2=None, op0=MULT)

        def image_planes(m):
            return planes[m // 2][:, :, (m % 2) * N : (m % 2 + 1) * N]

        def int_g(m):
            tile = xintp.tile([P, N, T], BF16, name="xint", align_bytes=64)
            xint[m] = tile
            nc.gpsimd.tensor_scalar(
                out=tile[:], in0=image_planes(m).rearrange("p t n -> p n t"),
                scalar1=1.0, scalar2=0.0, op0=MULT, op1=ADD,
            )

        def interleave(copy, dst, src):
            copy(out=dst.rearrange("p (c i) t -> p c t i", i=4), in_=src.rearrange("p t (c i) -> p c t i", i=4))

        def int_v(m):
            tile = xheadp.tile([P, N, T], BF16, name="xhead", align_bytes=64)
            xint[m] = tile
            interleave(nc.vector.tensor_copy, tile[:], image_planes(m))

        def quant_x(m):
            codes = xqp.tile([P, N], U32, name="x_mx", align_bytes=64)
            scales = xqp.tile([P, N], U8, name="x_mx_scales", align_bytes=64)
            xq[m] = (codes, scales)
            nc.vector.quantize_mx(out=codes[:].bitcast(FP8X4), scales=scales[:], in_=xint[m][:].rearrange("p n t -> p (n t)"))

        def mm(dst, w, t, m, lo, hi):
            codes, scales = xq[m]
            nc.tensor.matmul_mx(
                out=dst,
                lhsT=w_codes[:, w, t * P : (t + 1) * P].bitcast(FP8X4),
                lhsT_scale=w_scales[:, w, t * P : (t + 1) * P],
                rhs=codes[:, lo:hi].bitcast(FP8X4),
                rhs_scale=scales[:, lo:hi],
                start=True, stop=True,
            )

        def pe_key(m):
            for u in range(2):
                bank = psk.tile([P, 2, N], F32, name="kbank")
                ps["k", m, u] = bank
                for e in range(2):
                    mm(bank[:, e, :], 1, 2 * u + e, m, 0, N)

        def pe_query(m):
            for h in range(H):
                bank = psq.tile([P, T, P], F32, name="qbank")
                ps["q", m, h] = bank
                for t in range(T):
                    mm(bank[:, t, :], 0, t, m, h * P, (h + 1) * P)

        def key_exit(m):
            tile = kplp.tile([P, T, N], BF16, name="kplanes", align_bytes=64)
            kpl[m] = tile
            for t in range(T):
                nc.scalar.activation(out=tile[:, t, :], in_=ps["k", m, t // 2][:, t % 2, :], func=IDENT, bias=bias[:, 1, t : t + 1])

        def query_exit(m, h):
            if h == 0:
                tile = qkp.tile([P, 2, N, T], BF16, name="qk", align_bytes=64)
                qk[m] = tile
            nc.vector.tensor_tensor(
                out=qk[m][:, 0, h * P : (h + 1) * P, :],
                in0=ps["q", m, h][:].rearrange("p t n -> p n t"),
                in1=bias[:, 0, :].unsqueeze(1).to_broadcast([P, P, T]),
                op=ADD,
            )

        def key_int(copy, m, lo, hi):
            interleave(copy, qk[m][:, 1, lo:hi, :], kpl[m][:, :, lo:hi])

        def quant_qk(m):
            codes = qkcp.tile([P, 2 * N], U32, name="qk_mx", align_bytes=64)
            scales = qkcp.tile([P, 2 * N], U8, name="qk_mx_scales", align_bytes=64)
            qkc[m] = (codes, scales)
            nc.vector.quantize_mx(out=codes[:].bitcast(FP8X4), scales=scales[:], in_=qk[m][:].rearrange("p w n t -> p (w n t)"))

        def pe_out(m):
            codes, scales = qkc[m]
            bank = pso.tile([P, H, N], F32, name="obank")
            ps["o", m] = bank
            for h in range(H):
                nc.tensor.matmul_mx(
                    out=bank[:, h, :],
                    lhsT=codes[:, h * P : (h + 1) * P].bitcast(FP8X4),
                    lhsT_scale=scales[:, h * P : (h + 1) * P],
                    rhs=codes[:, N : 2 * N].bitcast(FP8X4),
                    rhs_scale=scales[:, N : 2 * N],
                    start=True, stop=True,
                )

        def out_exit(m):
            tile = outp.tile([P, H, N], F32, name="res", align_bytes=64)
            nc.vector.scalar_tensor_tensor(
                out=tile[:], in0=ps["o", m][:], scalar=SCALE, in1=fg[m // 4][:, m % 4, :, :], op0=MULT, op1=MULT,
            )
            nc.sync.dma_start(out=out[m].rearrange("(h p) m -> p h m", p=P), in_=tile[:])

        new_planes(0)
        widen_s(0, 0, 0, N)
        widen_s(0, 1, 0, N)
        widen_v(0, 2, 0, N)
        widen_v(0, 3, 0, N)
        int_v(0)
        nc.vector.tensor_copy(out=w_codes[:, 1, :].rearrange("p (t m) -> p t m", t=T), in_=w_raw[:, 1, :].rearrange("p (m t) -> p t m", t=T))
        quant_x(0)
        nc.vector.tensor_copy(
            out=w_scales[:].rearrange("p w (t m) -> p w t m", t=T), in_=s_raw[:].rearrange("p w (m t) -> p w t m", t=T))
        nc.vector.tensor_copy(out=w_codes[:, 0, :].rearrange("p (t m) -> p t m", t=T), in_=w_raw[:, 0, :].rearrange("p (m t) -> p t m", t=T))
        nc.vector.tensor_copy(out=bias[:, 1, :], in_=bk_b[:])
        nc.vector.tensor_copy(out=bias[:, 0, :], in_=bq_b[:])
        for t in range(T):
            widen_s(0, t, N, 2 * N)
        pe_key(0)
        pe_query(0)
        new_planes(1)
        for t in range(T):
            widen_v(1, t)
        int_g(2)
        int_v(1)
        quant_x(1)
        new_planes(2)

        pairs = B // 2
        for i in range(B + 2):
            if i + PREFETCH < B:
                load_x(i + PREFETCH)
            if i % 4 == 0 and i // 4 + 1 < B // 4:
                load_fg(i // 4 + 1)
            if i < B:
                key_exit(i)
                query_exit(i, 0)
                query_exit(i, 1)
            if i > 1:
                out_exit(i - 2)
            if i + 1 < B:
                pe_key(i + 1)
                pe_query(i + 1)
            if i < B:
                key_int(nc.vector.tensor_copy, i, 0, P)
            if 0 < i <= B:
                quant_qk(i - 1)
                pe_out(i - 1)
            if i + 2 < B:
                quant_x(i + 2)
            if i + 3 < B:
                int_g(i + 3)
            if i == 0:
                widen_s(2, 0)
                widen_s(2, 1)
            jw = (i + 4) // 2 if i % 2 == 0 else (i + 5) // 2
            if jw < pairs:
                if i % 2 == 1:
                    new_planes(jw)
                first = 2 if i % 2 == 0 else 0
                widen_s(jw, first)
                widen_s(jw, first + 1)
            if i < B:
                key_int(nc.scalar.copy, i, P, N)
